import numpy as np
import ml_dtypes


def mxq(x, axis, fmt="e4m3"):
    dtype, down = {"e4m3": (ml_dtypes.float8_e4m3fn, 7), "e5m2": (ml_dtypes.float8_e5m2, 14)}[fmt]
    v = np.moveaxis(np.asarray(x, np.float32).astype(ml_dtypes.bfloat16).astype(np.float64), axis, -1)
    blocks = v.reshape(v.shape[:-1] + (-1, 32))
    amax = np.abs(blocks).max(-1, keepdims=True)
    byte = np.maximum(np.where(amax > 0, np.frexp(amax)[1] - 1 + 127, 0) - down, 1)
    scale = np.exp2(byte - 127.0)
    codes = (blocks / scale).astype(np.float32).astype(dtype).astype(np.float64)
    return np.moveaxis((codes * scale).reshape(v.shape), -1, axis)


WIDE = False


def mx_kscale(k):
    if not WIDE:
        return np.ones(k)
    levels = np.array([10, -10, 5, -5, 0])
    if k % 512:
        return np.exp2(np.random.permutation(np.resize(levels, k // 32))).repeat(32)
    a = np.empty((k // 512, 16))
    for p in range(k // 512):
        a[p, :8] = np.random.permutation(np.resize(levels, 8))
        for g in range(8):
            far = levels[np.abs(levels - a[p, g]) >= 10]
            a[p, g + 8] = far[np.random.randint(len(far))]
    return np.exp2(a.ravel()).repeat(32)


BF16 = ml_dtypes.bfloat16


def bf(x):
    return np.asarray(x, np.float32).astype(BF16)


def f64(x):
    return np.asarray(x).astype(np.float64)


B, T, D = 4, 1024, 512
G = 0.78 * D ** 0.25


def setup_inputs():
    s = mx_kscale(D)
    n = np.random.standard_normal((B, T, D))
    n = n - n.mean(axis=1, keepdims=True)
    off = np.random.standard_normal((B, 1, D))
    y = G * n * s + off * np.minimum(s, 1.0)
    w = np.random.standard_normal((B, T, D))
    y_obs = np.random.standard_normal((B, T, D)) * 1.5
    return {"x": bf(np.concatenate([y, w, y_obs], axis=-1)),
            "kernel": bf(np.random.standard_normal((D, D)) * G / s[:, None])}


def reference(x, kernel):
    x = f64(x)
    kernel = f64(kernel)
    d = kernel.shape[0]
    y = x[:, :, :d]
    w = x[:, :, d:2 * d]
    y_obs = x[:, :, 2 * d:3 * d]
    intensity = np.exp(w)
    e = np.exp(w - w.max(axis=2, keepdims=True))
    sm = e / e.sum(axis=2, keepdims=True)
    mean = y.mean(axis=1, keepdims=True)
    u = sm * (y - mean)
    smooth = (mxq(u, 2, "e4m3") @ mxq(kernel, 0, "e4m3")) + mean
    y_trans = y_obs - smooth
    return np.concatenate([smooth, intensity, y_trans], axis=-1)

@@ -1,0 +1,375 @@
+from contextlib import ExitStack
+
+import concourse.mybir as mybir
+from concourse.masks import make_identity
+
+FP8X4 = mybir.dt.float8_e4m3fn_x4
+BF16 = mybir.dt.bfloat16
+F32 = mybir.dt.float32
+U32 = mybir.dt.uint32
+U8 = mybir.dt.uint8
+ALU = mybir.AluOpType
+ACT = mybir.ActivationFunctionType
+AX = mybir.AxisListType
+
+NB, T, D = 4, 1024, 512
+P = 128
+J = T // P
+KT = D // P
+NPAIR = NB * J // 2
+NQUAD = NB * J // 4
+ONES_N = 32
+
+FLOPS = 2 * NB * T * D * D
+
+
+def norm_on_vector(q, a):
+    return q < 2 or (a == 0 and q % 2 == 0)
+
+
+def tile_crosschannelinterp_t_kernel(tc, x, kernel, out):
+    nc = tc.nc
+    with ExitStack() as ctx:
+        const = ctx.enter_context(tc.tile_pool(name="const", bufs=1))
+        xpool = ctx.enter_context(tc.tile_pool(name="xpool", bufs=1))
+        opool = ctx.enter_context(tc.tile_pool(name="opool", bufs=5))
+        epool = ctx.enter_context(tc.tile_pool(name="epool", bufs=3))
+        work = ctx.enter_context(tc.tile_pool(name="work", bufs=2))
+        stat = ctx.enter_context(tc.tile_pool(name="stat", bufs=4))
+        ps_mean = ctx.enter_context(tc.psum_pool(name="ps_mean", bufs=1))
+        ps_yt = ctx.enter_context(tc.psum_pool(name="ps_yt", bufs=2))
+        ps_sm = ctx.enter_context(tc.psum_pool(name="ps_sm", bufs=3))
+        ps_p = ctx.enter_context(tc.psum_pool(name="ps_p", bufs=2))
+
+        xv = [x[b].rearrange("(p j) c -> p j c", j=J) for b in range(NB)]
+        ov = [out[b].rearrange("(p j) c -> p j c", j=J) for b in range(NB)]
+
+        kraw = const.tile([P, KT, D], BF16, name="kraw")
+        xb = [xpool.tile([P, J, 3 * D], BF16, name="x%d" % b) for b in range(NB)]
+
+        def load(b, j0, j1, c0, c1):
+            nc.sync.dma_start(out=xb[b][:, j0:j1, c0:c1], in_=xv[b][:, j0:j1, c0:c1])
+
+        load(0, 0, 4, D, 2 * D)
+        load(0, 0, 4, 0, D)
+        load(0, 4, 8, 0, D)
+        load(0, 4, 8, D, 2 * D)
+        nc.sync.dma_start(out=kraw[:], in_=kernel.rearrange("(p t) n -> p t n", t=KT))
+        load(1, 0, 4, 0, 3 * D)
+        load(0, 0, 8, 2 * D, 3 * D)
+        load(1, 4, 8, 0, 3 * D)
+        for b in range(2, NB):
+            load(b, 0, 4, 0, 3 * D)
+            load(b, 4, 8, 0, 3 * D)
+
+        ident_f = const.tile([P, P], F32, name="ident_f")
+        make_identity(nc, ident_f[:])
+        ones = const.tile([P, ONES_N], BF16, name="ones")
+        nc.vector.memset(ones[:], 1.0 / T)
+
+        kgrp = const.tile([P, D, KT], BF16, name="kgrp", align_bytes=64)
+        kcodes = const.tile([P, D], U32, name="kcodes", align_bytes=64)
+        kscl = const.tile([P, D], U8, name="kscl", align_bytes=64)
+
+        def kprep():
+            nc.vector.tensor_copy(out=kgrp[:].rearrange("p (c i) t -> p c t i", i=4),
+                                  in_=kraw[:].rearrange("p t (c i) -> p c t i", i=4))
+            nc.vector.quantize_mx(
+                out=kcodes[:].bitcast(FP8X4),
+                scales=kscl[:],
+                in_=kgrp[:].rearrange("p n t -> p (n t)"),
+            )
+
+        msum_t = {}
+        negmean = {}
+        rep_t = {}
+        mbc_t = {}
+        mean_sb = {}
+        tree_t = {}
+        negmax = {}
+        yt_t = {}
+        dt_t = {}
+        e_t = {}
+        ssum_t = {}
+        rs_t = {}
+        sm_t = {}
+        grp_t = {}
+        cod_t = {}
+        ob_t = {}
+        pp_t = {}
+
+        def mean_mm(b, half):
+            if half == 0:
+                msum_t[b] = ps_mean.tile([P, 2, KT, ONES_N], F32, name="msum", tag="mean")
+            for t in range(KT):
+                for j in range(4 * half, 4 * half + 4):
+                    nc.tensor.matmul(
+                        out=msum_t[b][:, half, t, :],
+                        lhsT=xb[b][:, j, t:D:KT],
+                        rhs=ones[:],
+                        start=(j == 4 * half),
+                        stop=(j == 4 * half + 3),
+                    )
+
+        def neg_mean(b):
+            nm = stat.tile([P, KT], F32, name="negmean")
+            nc.vector.tensor_reduce(out=nm[:], in_=msum_t[b][:, :, :, 0].rearrange("p h t -> p t h"),
+                                    axis=AX.X, op=ALU.add, negate=True)
+            negmean[b] = nm
+
+        def mean_rep(b):
+            rep = work.tile([P, KT, P], F32, name="rep")
+            nc.scalar.activation(out=rep[:], in_=negmean[b][:].unsqueeze(2).to_broadcast([P, KT, P]),
+                                 func=ACT.Copy, scale=-1.0)
+            rep_t[b] = rep
+
+        def mean_tr(b):
+            mbc = ps_mean.tile([P, KT, P], F32, name="mbc", tag="mean")
+            for t in range(KT):
+                nc.tensor.transpose(mbc[:, t, :], rep_t[b][:, t, :], ident_f[:])
+            mbc_t[b] = mbc
+
+        def mean_copy(b):
+            msb = work.tile([P, D], F32, name="msb")
+            nc.scalar.copy(out=msb[:].rearrange("p (c i t) -> p c t i", i=4, t=KT), in_=mbc_t[b][:].rearrange("p t (c i) -> p c t i", i=4))
+            mean_sb[b] = msb
+
+        def ytr(h, u):
+            b, j0 = h // 2, 4 * (h % 2)
+            yt = ps_yt.tile([P, 4 * P], F32, name="yt")
+            for a4 in range(4):
+                words = xb[b][:, j0 + a4, 0:D].bitcast(F32)
+                nc.tensor.transpose(yt[:, a4 * P:(a4 + 1) * P], words[:, u:D // 2:2], ident_f[:])
+            yt_t[(h, u)] = yt
+
+        def centre(h, u, on_vector=False):
+            b = h // 2
+            if u == 0:
+                dt_t[h] = work.tile([P, KT, 4 * P], F32, name="dT")
+            halves = yt_t[(h, u)][:].bitcast(BF16).rearrange("p (r e) -> p e r", e=2)
+            for e in range(2):
+                t = 2 * u + e
+                if on_vector:
+                    nc.vector.tensor_scalar(out=dt_t[h][:, t, :], in0=halves[:, e, :],
+                                            scalar1=negmean[b][:, t:t + 1], scalar2=None, op0=ALU.add)
+                else:
+                    nc.scalar.activation(out=dt_t[h][:, t, :], in_=halves[:, e, :], func=ACT.Identity,
+                                         bias=negmean[b][:, t:t + 1], scale=1.0)
+
+        def tree(h, level):
+            b, j0 = h // 2, 4 * (h % 2)
+            if level == 0:
+                t1 = work.tile([P, 4, 256], BF16, name="t1")
+                nc.vector.tensor_tensor(out=t1[:], in0=xb[b][:, j0:j0 + 4, D:D + 256],
+                                        in1=xb[b][:, j0:j0 + 4, D + 256:2 * D], op=ALU.max)
+                tree_t[h] = t1
+            elif level < 4:
+                w = 256 >> level
+                src = tree_t[h]
+                dst = work.tile([P, 4, w], BF16, name="t%d" % (level + 1))
+                nc.vector.tensor_tensor(out=dst[:], in0=src[:, :, 0:w], in1=src[:, :, w:2 * w], op=ALU.max)
+                tree_t[h] = dst
+            else:
+                nm = stat.tile([P, 4], F32, name="nm")
+                nc.vector.tensor_reduce(out=nm[:], in_=tree_t[h][:], axis=AX.X, op=ALU.max, negate=True)
+                negmax[h] = nm
+
+        def expo(q):
+            b, j0 = q // 4, 2 * (q % 4)
+            e_t[q] = epool.tile([P, 2, D], F32, name="e")
+            ssum_t[q] = stat.tile([P, 2], F32, name="ssum")
+            for a in range(2):
+                col = 2 * (q % 2) + a
+                nc.scalar.activation(
+                    out=e_t[q][:, a, :].rearrange("p (t c i) -> p c t i", t=KT, i=4),
+                    in_=xb[b][:, j0 + a, D:2 * D].rearrange("p (c i t) -> p c t i", i=4, t=KT),
+                    func=ACT.Exp,
+                    bias=negmax[q // 2][:, col:col + 1], scale=1.0, accum_out=ssum_t[q][:, a:a + 1],
+                )
+
+        def recip(q):
+            rs = stat.tile([P, 2], F32, name="rs")
+            nc.vector.reciprocal(out=rs[:], in_=ssum_t[q][:])
+            rs_t[q] = rs
+
+        def norm(q, a):
+            if norm_on_vector(q, a):
+                nc.vector.tensor_scalar(out=e_t[q][:, a, :], in0=e_t[q][:, a, :], scalar1=rs_t[q][:, a:a + 1],
+                                        scalar2=None, op0=ALU.mult)
+            else:
+                nc.scalar.activation(out=e_t[q][:, a, :], in_=e_t[q][:, a, :], func=ACT.Copy,
+                                     scale=rs_t[q][:, a:a + 1])
+
+        def smtr(q, a):
+            sm = ps_sm.tile([P, KT, P], F32, name="sm")
+            for t in range(KT):
+                nc.tensor.transpose(sm[:, t, :], e_t[q][:, a, t * P:(t + 1) * P], ident_f[:])
+            sm_t[(q, a)] = sm
+
+        def mult(q, a):
+            h = q // 2
+            if a == 0:
+                grp_t[q] = work.tile([P, 2, P, KT], BF16, name="grp", align_bytes=64)
+            c0 = (2 * (q % 2) + a) * P
+            nc.vector.tensor_tensor(
+                out=grp_t[q][:, a, :, :].rearrange("p (c i) t -> p c t i", i=4),
+                in0=dt_t[h][:, :, c0:c0 + P].rearrange("p t (c i) -> p c t i", i=4),
+                in1=sm_t[(q, a)][:].rearrange("p t (c i) -> p c t i", i=4),
+                op=ALU.mult,
+            )
+
+        def quant(q):
+            codes = work.tile([P, 2 * P], U32, name="codes", align_bytes=64)
+            scl = work.tile([P, 2 * P], U8, name="scl", align_bytes=64)
+            nc.vector.quantize_mx(
+                out=codes[:].bitcast(FP8X4), scales=scl[:],
+                in_=grp_t[q][:].rearrange("p a r t -> p (a r t)"),
+            )
+            cod_t[q] = (codes, scl)
+
+        def mxmm(q):
+            codes, scl = cod_t[q]
+            for a in range(2):
+                pp = ps_p.tile([P, D], F32, name="pp")
+                nc.tensor.matmul_mx(
+                    out=pp[:],
+                    lhsT=codes[:, a * P:(a + 1) * P].bitcast(FP8X4),
+                    lhsT_scale=scl[:, a * P:(a + 1) * P],
+                    rhs=kcodes[:].bitcast(FP8X4),
+                    rhs_scale=kscl[:],
+                    start=True, stop=True,
+                )
+                pp_t[(q, a)] = pp
+
+        def intensity(q):
+            b, j0 = q // 4, 2 * (q % 4)
+            ob = opool.tile([P, 2, 3 * D], F32, name="ob")
+            nc.scalar.activation(out=ob[:, :, D:2 * D], in_=xb[b][:, j0:j0 + 2, D:2 * D], func=ACT.Exp)
+            ob_t[q] = ob
+
+        def smooth(q, a):
+            nc.vector.tensor_tensor(out=ob_t[q][:, a, 0:D], in0=pp_t[(q, a)][:], in1=mean_sb[q // 4][:],
+                                    op=ALU.add)
+
+        def ytrans(q, a0, a1):
+            b, j0 = q // 4, 2 * (q % 4)
+            ob = ob_t[q]
+            nc.vector.tensor_tensor(out=ob[:, a0:a1, 2 * D:3 * D], in0=xb[b][:, j0 + a0:j0 + a1, 2 * D:3 * D],
+                                    in1=ob[:, a0:a1, 0:D], op=ALU.subtract)
+
+        def store(q, a0, a1, c0, c1):
+            b, j0 = q // 4, 2 * (q % 4)
+            nc.sync.dma_start(out=ov[b][:, j0 + a0:j0 + a1, c0:c1], in_=ob_t[q][:, a0:a1, c0:c1])
+
+        def live(q):
+            return 0 <= q < NPAIR
+
+        FINE = (NPAIR - 3, NPAIR - 2, NPAIR - 1)
+
+        intensity(0)
+        for level in range(5):
+            tree(0, level)
+        expo(0)
+        mean_mm(0, 0)
+        mean_mm(0, 1)
+        ytr(0, 0)
+        ytr(0, 1)
+        for level in range(5):
+            tree(1, level)
+        recip(0)
+        norm(0, 0)
+        norm(0, 1)
+        smtr(0, 0)
+        smtr(0, 1)
+        neg_mean(0)
+        mean_rep(0)
+        centre(0, 0)
+        centre(0, 1, on_vector=True)
+        expo(1)
+        mean_tr(0)
+        ytr(1, 0)
+        mean_copy(0)
+
+        for s in range(0, NPAIR + 1):
+            slots = []
+            if s % 2 == 0 and (s + 4) // 2 < NQUAD:
+                slots = [((s + 4) // 2, 0), ((s + 4) // 2, 1), ((s + 4) // 2, 2)]
+            if s % 2 == 1 and (s + 3) // 2 < NQUAD:
+                slots = [((s + 3) // 2, 3), ((s + 3) // 2, 4)]
+            bn = (s + 2) // 4
+            new_mean = s % 4 == 2 and bn < NB
+
+            if live(s):
+                mult(s, 0)
+            if live(s + 1):
+                recip(s + 1)
+                for a in range(2):
+                    if not norm_on_vector(s + 1, a):
+                        norm(s + 1, a)
+            if live(s):
+                mult(s, 1)
+            if live(s + 1):
+                for a in range(2):
+                    if norm_on_vector(s + 1, a):
+                        norm(s + 1, a)
+            if live(s + 1):
+                smtr(s + 1, 0)
+                smtr(s + 1, 1)
+            if len(slots) > 0:
+                tree(slots[0][0], slots[0][1])
+            if new_mean:
+                neg_mean(bn)
+                mean_rep(bn)
+            if live(s - 1):
+                smooth(s - 1, 0)
+            if len(slots) > 1:
+                tree(slots[1][0], slots[1][1])
+            if live(s - 1):
+                smooth(s - 1, 1)
+                if s - 1 in FINE:
+                    store(s - 1, 0, 2, 0, D)
+            if s == 0:
+                kprep()
+            if live(s):
+                quant(s)
+            if s - 1 in FINE:
+                ytrans(s - 1, 0, 1)
+                store(s - 1, 0, 1, 2 * D, 3 * D)
+            if len(slots) > 2:
+                tree(slots[2][0], slots[2][1])
+            if live(s - 1):
+                if s - 1 in FINE:
+                    ytrans(s - 1, 1, 2)
+                    store(s - 1, 1, 2, 2 * D, 3 * D)
+                else:
+                    ytrans(s - 1, 0, 2)
+                    store(s - 1, 0, 2, 0, 3 * D)
+            if s % 2 == 0 and 1 <= (s + 2) // 2 < NQUAD:
+                centre((s + 2) // 2, 0)
+            if s % 2 == 1 and 1 <= (s + 1) // 2 < NQUAD:
+                centre((s + 1) // 2, 1)
+            if live(s + 2):
+                expo(s + 2)
+            if 0 < s < FINE[0]:
+                intensity(s)
+            if s == FINE[0]:
+                intensity(s)
+                store(s, 0, 2, D, 2 * D)
+            if s == FINE[1]:
+                for q in FINE[1:]:
+                    intensity(q)
+                    store(q, 0, 2, D, 2 * D)
+            if s % 4 == 3 and (s + 1) // 4 < NB:
+                mean_copy((s + 1) // 4)
+            if s % 2 == 1 and 2 <= (s + 3) // 2 < NQUAD:
+                ytr((s + 3) // 2, 0)
+            if s % 2 == 0 and 1 <= (s + 2) // 2 < NQUAD:
+                ytr((s + 2) // 2, 1)
+            if s % 4 == 0 and (s + 4) // 4 < NB:
+                mean_mm((s + 4) // 4, 0)
+            if s % 4 == 1 and (s + 3) // 4 < NB:
+                mean_mm((s + 3) // 4, 1)
+            if new_mean:
+                mean_tr(bn)
+            if live(s):
+                mxmm(s)

@@ -23,8 +23,7 @@ ONES_N = 32
 FLOPS = 2 * NB * T * D * D
 
 
-def norm_on_vector(q, a):
-    return q < 2 or (a == 0 and q % 2 == 0)
+GY = 256
 
 
 def tile_crosschannelinterp_t_kernel(tc, x, kernel, out):
@@ -32,7 +31,7 @@ def tile_crosschannelinterp_t_kernel(tc, x, kernel, out):
     with ExitStack() as ctx:
         const = ctx.enter_context(tc.tile_pool(name="const", bufs=1))
         xpool = ctx.enter_context(tc.tile_pool(name="xpool", bufs=1))
-        opool = ctx.enter_context(tc.tile_pool(name="opool", bufs=5))
+        opool = ctx.enter_context(tc.tile_pool(name="opool", bufs=6))
         epool = ctx.enter_context(tc.tile_pool(name="epool", bufs=3))
         work = ctx.enter_context(tc.tile_pool(name="work", bufs=2))
         stat = ctx.enter_context(tc.tile_pool(name="stat", bufs=4))
@@ -40,27 +39,39 @@ def tile_crosschannelinterp_t_kernel(tc, x, kernel, out):
         ps_yt = ctx.enter_context(tc.psum_pool(name="ps_yt", bufs=2))
         ps_sm = ctx.enter_context(tc.psum_pool(name="ps_sm", bufs=3))
         ps_p = ctx.enter_context(tc.psum_pool(name="ps_p", bufs=2))
+        ctx.enter_context(tc.manual_schedule())
 
         xv = [x[b].rearrange("(p j) c -> p j c", j=J) for b in range(NB)]
         ov = [out[b].rearrange("(p j) c -> p j c", j=J) for b in range(NB)]
 
         kraw = const.tile([P, KT, D], BF16, name="kraw")
-        xb = [xpool.tile([P, J, 3 * D], BF16, name="x%d" % b) for b in range(NB)]
+        first = [xpool.tile([P, J, D], BF16, name="first%d" % i) for i in range(3)]
+        xb = [None] + [xpool.tile([P, J, 3 * D], BF16, name="x%d" % b) for b in range(1, NB)]
 
-        def load(b, j0, j1, c0, c1):
-            nc.sync.dma_start(out=xb[b][:, j0:j1, c0:c1], in_=xv[b][:, j0:j1, c0:c1])
+        def block(b, i):
+            return first[i][:] if b == 0 else xb[b][:, :, i * D:(i + 1) * D]
 
-        load(0, 0, 4, D, 2 * D)
-        load(0, 0, 4, 0, D)
-        load(0, 4, 8, 0, D)
-        load(0, 4, 8, D, 2 * D)
+        yb = [block(b, 0) for b in range(NB)]
+        wb = [block(b, 1) for b in range(NB)]
+        ob_in = [block(b, 2) for b in range(NB)]
+
+        def load_first(i, j0, j1):
+            nc.sync.dma_start(out=first[i][:, j0:j1, :], in_=xv[0][:, j0:j1, i * D:(i + 1) * D])
+
+        def load(b, j0, j1):
+            nc.sync.dma_start(out=xb[b][:, j0:j1, :], in_=xv[b][:, j0:j1, :])
+
+        load_first(1, 0, 4)
+        load_first(1, 4, 8)
+        load_first(0, 0, 4)
+        load_first(0, 4, 8)
         nc.sync.dma_start(out=kraw[:], in_=kernel.rearrange("(p t) n -> p t n", t=KT))
-        load(1, 0, 4, 0, 3 * D)
-        load(0, 0, 8, 2 * D, 3 * D)
-        load(1, 4, 8, 0, 3 * D)
+        load(1, 0, 4)
+        load_first(2, 0, 8)
+        load(1, 4, 8)
         for b in range(2, NB):
-            load(b, 0, 4, 0, 3 * D)
-            load(b, 4, 8, 0, 3 * D)
+            load(b, 0, 4)
+            load(b, 4, 8)
 
         ident_f = const.tile([P, P], F32, name="ident_f")
         make_identity(nc, ident_f[:])
@@ -105,7 +116,7 @@ def tile_crosschannelinterp_t_kernel(tc, x, kernel, out):
                 for j in range(4 * half, 4 * half + 4):
                     nc.tensor.matmul(
                         out=msum_t[b][:, half, t, :],
-                        lhsT=xb[b][:, j, t:D:KT],
+                        lhsT=yb[b][:, j, t:D:KT],
                         rhs=ones[:],
                         start=(j == 4 * half),
                         stop=(j == 4 * half + 3),
@@ -138,7 +149,7 @@ def tile_crosschannelinterp_t_kernel(tc, x, kernel, out):
             b, j0 = h // 2, 4 * (h % 2)
             yt = ps_yt.tile([P, 4 * P], F32, name="yt")
             for a4 in range(4):
-                words = xb[b][:, j0 + a4, 0:D].bitcast(F32)
+                words = yb[b][:, j0 + a4, 0:D].bitcast(F32)
                 nc.tensor.transpose(yt[:, a4 * P:(a4 + 1) * P], words[:, u:D // 2:2], ident_f[:])
             yt_t[(h, u)] = yt
 
@@ -160,8 +171,8 @@ def tile_crosschannelinterp_t_kernel(tc, x, kernel, out):
             b, j0 = h // 2, 4 * (h % 2)
             if level == 0:
                 t1 = work.tile([P, 4, 256], BF16, name="t1")
-                nc.vector.tensor_tensor(out=t1[:], in0=xb[b][:, j0:j0 + 4, D:D + 256],
-                                        in1=xb[b][:, j0:j0 + 4, D + 256:2 * D], op=ALU.max)
+                nc.vector.tensor_tensor(out=t1[:], in0=wb[b][:, j0:j0 + 4, 0:256],
+                                        in1=wb[b][:, j0:j0 + 4, 256:D], op=ALU.max)
                 tree_t[h] = t1
             elif level < 4:
                 w = 256 >> level
@@ -182,7 +193,7 @@ def tile_crosschannelinterp_t_kernel(tc, x, kernel, out):
                 col = 2 * (q % 2) + a
                 nc.scalar.activation(
                     out=e_t[q][:, a, :].rearrange("p (t c i) -> p c t i", t=KT, i=4),
-                    in_=xb[b][:, j0 + a, D:2 * D].rearrange("p (c i t) -> p c t i", i=4, t=KT),
+                    in_=wb[b][:, j0 + a, :].rearrange("p (c i t) -> p c t i", i=4, t=KT),
                     func=ACT.Exp,
                     bias=negmax[q // 2][:, col:col + 1], scale=1.0, accum_out=ssum_t[q][:, a:a + 1],
                 )
@@ -193,9 +204,12 @@ def tile_crosschannelinterp_t_kernel(tc, x, kernel, out):
             rs_t[q] = rs
 
         def norm(q, a):
-            if norm_on_vector(q, a):
+            if q < 2:
                 nc.vector.tensor_scalar(out=e_t[q][:, a, :], in0=e_t[q][:, a, :], scalar1=rs_t[q][:, a:a + 1],
                                         scalar2=None, op0=ALU.mult)
+            elif a == 0:
+                nc.gpsimd.tensor_scalar(out=e_t[q][:, a, :], in0=e_t[q][:, a, :], scalar1=rs_t[q][:, a:a + 1],
+                                        scalar2=0.0, op0=ALU.mult, op1=ALU.add)
             else:
                 nc.scalar.activation(out=e_t[q][:, a, :], in_=e_t[q][:, a, :], func=ACT.Copy,
                                      scale=rs_t[q][:, a:a + 1])
@@ -244,18 +258,18 @@ def tile_crosschannelinterp_t_kernel(tc, x, kernel, out):
         def intensity(q):
             b, j0 = q // 4, 2 * (q % 4)
             ob = opool.tile([P, 2, 3 * D], F32, name="ob")
-            nc.scalar.activation(out=ob[:, :, D:2 * D], in_=xb[b][:, j0:j0 + 2, D:2 * D], func=ACT.Exp)
+            nc.scalar.activation(out=ob[:, :, D:2 * D], in_=wb[b][:, j0:j0 + 2, :], func=ACT.Exp)
             ob_t[q] = ob
 
         def smooth(q, a):
             nc.vector.tensor_tensor(out=ob_t[q][:, a, 0:D], in0=pp_t[(q, a)][:], in1=mean_sb[q // 4][:],
                                     op=ALU.add)
 
-        def ytrans(q, a0, a1):
+        def ytrans(eng, q, a0, a1, c0, c1):
             b, j0 = q // 4, 2 * (q % 4)
             ob = ob_t[q]
-            nc.vector.tensor_tensor(out=ob[:, a0:a1, 2 * D:3 * D], in0=xb[b][:, j0 + a0:j0 + a1, 2 * D:3 * D],
-                                    in1=ob[:, a0:a1, 0:D], op=ALU.subtract)
+            eng.tensor_tensor(out=ob[:, a0:a1, 2 * D + c0:2 * D + c1], in0=ob_in[b][:, j0 + a0:j0 + a1, c0:c1],
+                              in1=ob[:, a0:a1, c0:c1], op=ALU.subtract)
 
         def store(q, a0, a1, c0, c1):
             b, j0 = q // 4, 2 * (q % 4)
@@ -274,21 +288,23 @@ def tile_crosschannelinterp_t_kernel(tc, x, kernel, out):
         mean_mm(0, 1)
         ytr(0, 0)
         ytr(0, 1)
-        for level in range(5):
-            tree(1, level)
+        tree(1, 0)
+        tree(1, 1)
+        neg_mean(0)
         recip(0)
         norm(0, 0)
         norm(0, 1)
         smtr(0, 0)
         smtr(0, 1)
-        neg_mean(0)
-        mean_rep(0)
         centre(0, 0)
         centre(0, 1, on_vector=True)
         expo(1)
+        mean_rep(0)
         mean_tr(0)
         ytr(1, 0)
         mean_copy(0)
+        for level in range(2, 5):
+            tree(1, level)
 
         for s in range(0, NPAIR + 1):
             slots = []
@@ -299,51 +315,45 @@ def tile_crosschannelinterp_t_kernel(tc, x, kernel, out):
             bn = (s + 2) // 4
             new_mean = s % 4 == 2 and bn < NB
 
-            if live(s):
-                mult(s, 0)
             if live(s + 1):
                 recip(s + 1)
-                for a in range(2):
-                    if not norm_on_vector(s + 1, a):
-                        norm(s + 1, a)
-            if live(s):
-                mult(s, 1)
-            if live(s + 1):
-                for a in range(2):
-                    if norm_on_vector(s + 1, a):
-                        norm(s + 1, a)
-            if live(s + 1):
-                smtr(s + 1, 0)
-                smtr(s + 1, 1)
-            if len(slots) > 0:
-                tree(slots[0][0], slots[0][1])
+                norm(s + 1, 0)
+                norm(s + 1, 1)
             if new_mean:
                 neg_mean(bn)
                 mean_rep(bn)
+            if live(s):
+                mult(s, 0)
+                mult(s, 1)
             if live(s - 1):
                 smooth(s - 1, 0)
-            if len(slots) > 1:
-                tree(slots[1][0], slots[1][1])
-            if live(s - 1):
                 smooth(s - 1, 1)
                 if s - 1 in FINE:
                     store(s - 1, 0, 2, 0, D)
+            if 0 <= s - 2 < FINE[0]:
+                ytrans(nc.gpsimd, s - 2, 0, 2, 0, GY)
+                store(s - 2, 0, 2, 0, 3 * D)
+            if live(s + 1):
+                smtr(s + 1, 0)
+                smtr(s + 1, 1)
             if s == 0:
                 kprep()
             if live(s):
                 quant(s)
+            if len(slots) > 0:
+                tree(slots[0][0], slots[0][1])
             if s - 1 in FINE:
-                ytrans(s - 1, 0, 1)
+                ytrans(nc.vector, s - 1, 0, 1, 0, D)
                 store(s - 1, 0, 1, 2 * D, 3 * D)
+            elif live(s - 1):
+                ytrans(nc.vector, s - 1, 0, 2, GY, D)
+            if len(slots) > 1:
+                tree(slots[1][0], slots[1][1])
+            if s - 1 in FINE:
+                ytrans(nc.vector, s - 1, 1, 2, 0, D)
+                store(s - 1, 1, 2, 2 * D, 3 * D)
             if len(slots) > 2:
                 tree(slots[2][0], slots[2][1])
-            if live(s - 1):
-                if s - 1 in FINE:
-                    ytrans(s - 1, 1, 2)
-                    store(s - 1, 1, 2, 2 * D, 3 * D)
-                else:
-                    ytrans(s - 1, 0, 2)
-                    store(s - 1, 0, 2, 0, 3 * D)
             if s % 2 == 0 and 1 <= (s + 2) // 2 < NQUAD:
                 centre((s + 2) // 2, 0)
             if s % 2 == 1 and 1 <= (s + 1) // 2 < NQUAD:

@@ -82,9 +82,11 @@ def tile_crosschannelinterp_t_kernel(tc, x, kernel, out):
         kcodes = const.tile([P, D], U32, name="kcodes", align_bytes=64)
         kscl = const.tile([P, D], U8, name="kscl", align_bytes=64)
 
-        def kprep():
+        def kgroup():
             nc.vector.tensor_copy(out=kgrp[:].rearrange("p (c i) t -> p c t i", i=4),
                                   in_=kraw[:].rearrange("p t (c i) -> p c t i", i=4))
+
+        def kquant():
             nc.vector.quantize_mx(
                 out=kcodes[:].bitcast(FP8X4),
                 scales=kscl[:],
@@ -204,7 +206,7 @@ def tile_crosschannelinterp_t_kernel(tc, x, kernel, out):
             rs_t[q] = rs
 
         def norm(q, a):
-            if q < 2:
+            if q < 2 or (a == 1 and q % 2 == 1):
                 nc.vector.tensor_scalar(out=e_t[q][:, a, :], in0=e_t[q][:, a, :], scalar1=rs_t[q][:, a:a + 1],
                                         scalar2=None, op0=ALU.mult)
             elif a == 0:
@@ -290,39 +292,42 @@ def tile_crosschannelinterp_t_kernel(tc, x, kernel, out):
         ytr(0, 1)
         tree(1, 0)
         tree(1, 1)
-        neg_mean(0)
         recip(0)
         norm(0, 0)
         norm(0, 1)
-        smtr(0, 0)
-        smtr(0, 1)
+        tree(1, 2)
+        neg_mean(0)
         centre(0, 0)
         centre(0, 1, on_vector=True)
+        smtr(0, 0)
+        smtr(0, 1)
         expo(1)
         mean_rep(0)
         mean_tr(0)
         ytr(1, 0)
         mean_copy(0)
-        for level in range(2, 5):
-            tree(1, level)
 
         for s in range(0, NPAIR + 1):
             slots = []
             if s % 2 == 0 and (s + 4) // 2 < NQUAD:
-                slots = [((s + 4) // 2, 0), ((s + 4) // 2, 1), ((s + 4) // 2, 2)]
+                slots = [((s + 4) // 2, 0), ((s + 4) // 2, 1)]
             if s % 2 == 1 and (s + 3) // 2 < NQUAD:
-                slots = [((s + 3) // 2, 3), ((s + 3) // 2, 4)]
+                slots = [((s + 3) // 2, 2), ((s + 3) // 2, 3), ((s + 3) // 2, 4)]
             bn = (s + 2) // 4
             new_mean = s % 4 == 2 and bn < NB
 
+            if s == 0:
+                mult(0, 0)
+                mult(0, 1)
             if live(s + 1):
                 recip(s + 1)
                 norm(s + 1, 0)
-                norm(s + 1, 1)
+                if s == 0 or s % 2 == 1:
+                    norm(s + 1, 1)
             if new_mean:
                 neg_mean(bn)
                 mean_rep(bn)
-            if live(s):
+            if 0 < s < NPAIR:
                 mult(s, 0)
                 mult(s, 1)
             if live(s - 1):
@@ -335,25 +340,29 @@ def tile_crosschannelinterp_t_kernel(tc, x, kernel, out):
                 store(s - 2, 0, 2, 0, 3 * D)
             if live(s + 1):
                 smtr(s + 1, 0)
-                smtr(s + 1, 1)
             if s == 0:
-                kprep()
+                tree(1, 3)
+                kgroup()
+                tree(1, 4)
+                kquant()
+            if len(slots) > 2:
+                tree(*slots.pop(0))
             if live(s):
                 quant(s)
+            if 0 < s < NPAIR - 1 and s % 2 == 0:
+                norm(s + 1, 1)
             if len(slots) > 0:
-                tree(slots[0][0], slots[0][1])
+                tree(*slots[0])
             if s - 1 in FINE:
                 ytrans(nc.vector, s - 1, 0, 1, 0, D)
                 store(s - 1, 0, 1, 2 * D, 3 * D)
             elif live(s - 1):
                 ytrans(nc.vector, s - 1, 0, 2, GY, D)
             if len(slots) > 1:
-                tree(slots[1][0], slots[1][1])
+                tree(*slots[1])
             if s - 1 in FINE:
                 ytrans(nc.vector, s - 1, 1, 2, 0, D)
                 store(s - 1, 1, 2, 2 * D, 3 * D)
-            if len(slots) > 2:
-                tree(slots[2][0], slots[2][1])
             if s % 2 == 0 and 1 <= (s + 2) // 2 < NQUAD:
                 centre((s + 2) // 2, 0)
             if s % 2 == 1 and 1 <= (s + 1) // 2 < NQUAD:
@@ -381,5 +390,7 @@ def tile_crosschannelinterp_t_kernel(tc, x, kernel, out):
                 mean_mm((s + 3) // 4, 1)
             if new_mean:
                 mean_tr(bn)
+            if live(s + 1):
+                smtr(s + 1, 1)
             if live(s):
                 mxmm(s)

@@ -23,6 +23,7 @@ ONES_N = 32
 FLOPS = 2 * NB * T * D * D
 
 
+SPLIT = NPAIR // 2
 GY = 256
 
 
@@ -61,17 +62,18 @@ def tile_crosschannelinterp_t_kernel(tc, x, kernel, out):
         def load(b, j0, j1):
             nc.sync.dma_start(out=xb[b][:, j0:j1, :], in_=xv[b][:, j0:j1, :])
 
-        load_first(1, 0, 4)
-        load_first(1, 4, 8)
+        load_first(1, 0, 2)
         load_first(0, 0, 4)
         load_first(0, 4, 8)
+        load_first(1, 2, 4)
+        load_first(1, 4, 8)
         nc.sync.dma_start(out=kraw[:], in_=kernel.rearrange("(p t) n -> p t n", t=KT))
         load(1, 0, 4)
-        load_first(2, 0, 8)
+        load_first(2, 0, 4)
         load(1, 4, 8)
+        load_first(2, 4, 8)
         for b in range(2, NB):
-            load(b, 0, 4)
-            load(b, 4, 8)
+            load(b, 0, 8)
 
         ident_f = const.tile([P, P], F32, name="ident_f")
         make_identity(nc, ident_f[:])
@@ -95,9 +97,8 @@ def tile_crosschannelinterp_t_kernel(tc, x, kernel, out):
 
         msum_t = {}
         negmean = {}
-        rep_t = {}
         mbc_t = {}
-        mean_sb = {}
+        negmean_sb = {}
         tree_t = {}
         negmax = {}
         yt_t = {}
@@ -130,22 +131,16 @@ def tile_crosschannelinterp_t_kernel(tc, x, kernel, out):
                                     axis=AX.X, op=ALU.add, negate=True)
             negmean[b] = nm
 
-        def mean_rep(b):
-            rep = work.tile([P, KT, P], F32, name="rep")
-            nc.scalar.activation(out=rep[:], in_=negmean[b][:].unsqueeze(2).to_broadcast([P, KT, P]),
-                                 func=ACT.Copy, scale=-1.0)
-            rep_t[b] = rep
-
         def mean_tr(b):
             mbc = ps_mean.tile([P, KT, P], F32, name="mbc", tag="mean")
             for t in range(KT):
-                nc.tensor.transpose(mbc[:, t, :], rep_t[b][:, t, :], ident_f[:])
+                nc.tensor.transpose(mbc[:, t, :], negmean[b][:, t:t + 1].to_broadcast([P, P]), ident_f[:])
             mbc_t[b] = mbc
 
         def mean_copy(b):
             msb = work.tile([P, D], F32, name="msb")
             nc.scalar.copy(out=msb[:].rearrange("p (c i t) -> p c t i", i=4, t=KT), in_=mbc_t[b][:].rearrange("p t (c i) -> p c t i", i=4))
-            mean_sb[b] = msb
+            negmean_sb[b] = msb
 
         def ytr(h, u):
             b, j0 = h // 2, 4 * (h % 2)
@@ -155,49 +150,54 @@ def tile_crosschannelinterp_t_kernel(tc, x, kernel, out):
                 nc.tensor.transpose(yt[:, a4 * P:(a4 + 1) * P], words[:, u:D // 2:2], ident_f[:])
             yt_t[(h, u)] = yt
 
-        def centre(h, u, on_vector=False):
+        def centre(h, t, on_vector=False):
             b = h // 2
-            if u == 0:
+            if t == 0:
                 dt_t[h] = work.tile([P, KT, 4 * P], F32, name="dT")
-            halves = yt_t[(h, u)][:].bitcast(BF16).rearrange("p (r e) -> p e r", e=2)
-            for e in range(2):
-                t = 2 * u + e
-                if on_vector:
-                    nc.vector.tensor_scalar(out=dt_t[h][:, t, :], in0=halves[:, e, :],
-                                            scalar1=negmean[b][:, t:t + 1], scalar2=None, op0=ALU.add)
-                else:
-                    nc.scalar.activation(out=dt_t[h][:, t, :], in_=halves[:, e, :], func=ACT.Identity,
-                                         bias=negmean[b][:, t:t + 1], scale=1.0)
+            src = yt_t[(h, t // 2)][:].bitcast(BF16).rearrange("p (r e) -> p e r", e=2)[:, t % 2, :]
+            if on_vector:
+                nc.vector.tensor_scalar(out=dt_t[h][:, t, :], in0=src,
+                                        scalar1=negmean[b][:, t:t + 1], scalar2=None, op0=ALU.add)
+            else:
+                nc.scalar.activation(out=dt_t[h][:, t, :], in_=src, func=ACT.Identity,
+                                     bias=negmean[b][:, t:t + 1], scale=1.0)
 
-        def tree(h, level):
-            b, j0 = h // 2, 4 * (h % 2)
+        def centre_two(h, u):
+            for t in (2 * u, 2 * u + 1):
+                centre(h, t)
+
+        def tree(h, level, half=None):
+            b, j0, n = h // 2, 4 * (h % 2), 4
+            if half is not None:
+                j0, n = j0 + 2 * half, 2
             if level == 0:
                 t1 = work.tile([P, 4, 256], BF16, name="t1")
-                nc.vector.tensor_tensor(out=t1[:], in0=wb[b][:, j0:j0 + 4, 0:256],
-                                        in1=wb[b][:, j0:j0 + 4, 256:D], op=ALU.max)
+                nc.vector.tensor_tensor(out=t1[:, 0:n, :], in0=wb[b][:, j0:j0 + n, 0:256],
+                                        in1=wb[b][:, j0:j0 + n, 256:D], op=ALU.max)
                 tree_t[h] = t1
             elif level < 4:
                 w = 256 >> level
                 src = tree_t[h]
                 dst = work.tile([P, 4, w], BF16, name="t%d" % (level + 1))
-                nc.vector.tensor_tensor(out=dst[:], in0=src[:, :, 0:w], in1=src[:, :, w:2 * w], op=ALU.max)
+                nc.vector.tensor_tensor(out=dst[:, 0:n, :], in0=src[:, 0:n, 0:w], in1=src[:, 0:n, w:2 * w],
+                                        op=ALU.max)
                 tree_t[h] = dst
             else:
                 nm = stat.tile([P, 4], F32, name="nm")
-                nc.vector.tensor_reduce(out=nm[:], in_=tree_t[h][:], axis=AX.X, op=ALU.max, negate=True)
-                negmax[h] = nm
+                nc.vector.tensor_reduce(out=nm[:, 0:n], in_=tree_t[h][:, 0:n, :], axis=AX.X, op=ALU.max, negate=True)
+                for i in range(n // 2):
+                    negmax[4 * b + j0 // 2 + i] = nm[:, 2 * i:2 * i + 2]
 
         def expo(q):
             b, j0 = q // 4, 2 * (q % 4)
             e_t[q] = epool.tile([P, 2, D], F32, name="e")
             ssum_t[q] = stat.tile([P, 2], F32, name="ssum")
             for a in range(2):
-                col = 2 * (q % 2) + a
                 nc.scalar.activation(
                     out=e_t[q][:, a, :].rearrange("p (t c i) -> p c t i", t=KT, i=4),
                     in_=wb[b][:, j0 + a, :].rearrange("p (c i t) -> p c t i", i=4, t=KT),
                     func=ACT.Exp,
-                    bias=negmax[q // 2][:, col:col + 1], scale=1.0, accum_out=ssum_t[q][:, a:a + 1],
+                    bias=negmax[q][:, a:a + 1], scale=1.0, accum_out=ssum_t[q][:, a:a + 1],
                 )
 
         def recip(q):
@@ -264,8 +264,8 @@ def tile_crosschannelinterp_t_kernel(tc, x, kernel, out):
             ob_t[q] = ob
 
         def smooth(q, a):
-            nc.vector.tensor_tensor(out=ob_t[q][:, a, 0:D], in0=pp_t[(q, a)][:], in1=mean_sb[q // 4][:],
-                                    op=ALU.add)
+            nc.vector.tensor_tensor(out=ob_t[q][:, a, 0:D], in0=pp_t[(q, a)][:], in1=negmean_sb[q // 4][:],
+                                    op=ALU.subtract)
 
         def ytrans(eng, q, a0, a1, c0, c1):
             b, j0 = q // 4, 2 * (q % 4)
@@ -280,34 +280,58 @@ def tile_crosschannelinterp_t_kernel(tc, x, kernel, out):
         def live(q):
             return 0 <= q < NPAIR
 
-        FINE = (NPAIR - 3, NPAIR - 2, NPAIR - 1)
+        LATE = NPAIR - 3
 
         intensity(0)
         for level in range(5):
-            tree(0, level)
+            tree(0, level, 0)
         expo(0)
         mean_mm(0, 0)
         mean_mm(0, 1)
         ytr(0, 0)
         ytr(0, 1)
-        tree(1, 0)
-        tree(1, 1)
+        tree(0, 0, 1)
+        neg_mean(0)
+        tree(0, 1, 1)
         recip(0)
         norm(0, 0)
         norm(0, 1)
-        tree(1, 2)
-        neg_mean(0)
-        centre(0, 0)
-        centre(0, 1, on_vector=True)
+        for level in range(2, 5):
+            tree(0, level, 1)
+        centre_two(0, 0)
+        centre(0, 2)
+        centre(0, 3, on_vector=True)
         smtr(0, 0)
         smtr(0, 1)
         expo(1)
-        mean_rep(0)
-        mean_tr(0)
         ytr(1, 0)
+        mean_tr(0)
         mean_copy(0)
 
-        for s in range(0, NPAIR + 1):
+        mult(0, 0)
+        mult(0, 1)
+        centre_two(1, 0)
+        recip(1)
+        norm(1, 0)
+        tree(1, 0)
+        norm(1, 1)
+        smtr(1, 0)
+        tree(1, 1)
+        quant(0)
+        tree(1, 2)
+        tree(2, 0)
+        tree(1, 3)
+        tree(2, 1)
+        tree(1, 4)
+        kgroup()
+        kquant()
+        expo(2)
+        ytr(1, 1)
+        mean_mm(1, 0)
+        smtr(1, 1)
+        mxmm(0)
+
+        for s in range(1, NPAIR + 1):
             slots = []
             if s % 2 == 0 and (s + 4) // 2 < NQUAD:
                 slots = [((s + 4) // 2, 0), ((s + 4) // 2, 1)]
@@ -316,74 +340,57 @@ def tile_crosschannelinterp_t_kernel(tc, x, kernel, out):
             bn = (s + 2) // 4
             new_mean = s % 4 == 2 and bn < NB
 
-            if s == 0:
-                mult(0, 0)
-                mult(0, 1)
             if live(s + 1):
                 recip(s + 1)
                 norm(s + 1, 0)
-                if s == 0 or s % 2 == 1:
-                    norm(s + 1, 1)
             if new_mean:
                 neg_mean(bn)
-                mean_rep(bn)
-            if 0 < s < NPAIR:
+            if s % 4 == 3 and (s + 1) // 4 < NB:
+                mean_copy((s + 1) // 4)
+            if live(s + 2):
+                expo(s + 2)
+            if s % 2 == 1 and live(s + 1):
+                norm(s + 1, 1)
+            if s % 2 == 0 and (s + 2) // 2 < NQUAD:
+                centre_two((s + 2) // 2, 0)
+            if s % 2 == 1 and (s + 1) // 2 < NQUAD:
+                centre_two((s + 1) // 2, 1)
+            if live(s):
                 mult(s, 0)
                 mult(s, 1)
-            if live(s - 1):
-                smooth(s - 1, 0)
-                smooth(s - 1, 1)
-                if s - 1 in FINE:
-                    store(s - 1, 0, 2, 0, D)
-            if 0 <= s - 2 < FINE[0]:
+            smooth(s - 1, 0)
+            smooth(s - 1, 1)
+            if s - 1 >= SPLIT:
+                store(s - 1, 0, 2, 0, 2 * D)
+            if 0 <= s - 2 < LATE:
                 ytrans(nc.gpsimd, s - 2, 0, 2, 0, GY)
-                store(s - 2, 0, 2, 0, 3 * D)
-            if live(s + 1):
-                smtr(s + 1, 0)
-            if s == 0:
-                tree(1, 3)
-                kgroup()
-                tree(1, 4)
-                kquant()
+                store(s - 2, 0, 2, 2 * D if s - 2 >= SPLIT else 0, 3 * D)
             if len(slots) > 2:
                 tree(*slots.pop(0))
             if live(s):
                 quant(s)
-            if 0 < s < NPAIR - 1 and s % 2 == 0:
+            if s % 2 == 0 and s < NPAIR - 1:
                 norm(s + 1, 1)
             if len(slots) > 0:
                 tree(*slots[0])
-            if s - 1 in FINE:
-                ytrans(nc.vector, s - 1, 0, 1, 0, D)
-                store(s - 1, 0, 1, 2 * D, 3 * D)
-            elif live(s - 1):
+            if s - 1 >= LATE:
+                ytrans(nc.vector, s - 1, 0, 2, 0, D)
+                store(s - 1, 0, 2, 2 * D, 3 * D)
+            else:
                 ytrans(nc.vector, s - 1, 0, 2, GY, D)
             if len(slots) > 1:
                 tree(*slots[1])
-            if s - 1 in FINE:
-                ytrans(nc.vector, s - 1, 1, 2, 0, D)
-                store(s - 1, 1, 2, 2 * D, 3 * D)
-            if s % 2 == 0 and 1 <= (s + 2) // 2 < NQUAD:
-                centre((s + 2) // 2, 0)
-            if s % 2 == 1 and 1 <= (s + 1) // 2 < NQUAD:
-                centre((s + 1) // 2, 1)
-            if live(s + 2):
-                expo(s + 2)
-            if 0 < s < FINE[0]:
+            if s < NPAIR - 2:
                 intensity(s)
-            if s == FINE[0]:
+            elif s == NPAIR - 2:
                 intensity(s)
-                store(s, 0, 2, D, 2 * D)
-            if s == FINE[1]:
-                for q in FINE[1:]:
-                    intensity(q)
-                    store(q, 0, 2, D, 2 * D)
-            if s % 4 == 3 and (s + 1) // 4 < NB:
-                mean_copy((s + 1) // 4)
+                intensity(s + 1)
             if s % 2 == 1 and 2 <= (s + 3) // 2 < NQUAD:
                 ytr((s + 3) // 2, 0)
-            if s % 2 == 0 and 1 <= (s + 2) // 2 < NQUAD:
+            if s % 2 == 0 and (s + 2) // 2 < NQUAD:
                 ytr((s + 2) // 2, 1)
+            if live(s + 1):
+                smtr(s + 1, 0)
             if s % 4 == 0 and (s + 4) // 4 < NB:
                 mean_mm((s + 4) // 4, 0)
             if s % 4 == 1 and (s + 3) // 4 < NB:

@@ -23,7 +23,8 @@ ONES_N = 32
 FLOPS = 2 * NB * T * D * D
 
 
-SPLIT = NPAIR // 2
+LATE = NPAIR - 3
+SPLIT = range(NPAIR // 2, LATE)
 GY = 256
 
 
@@ -85,8 +86,8 @@ def tile_crosschannelinterp_t_kernel(tc, x, kernel, out):
         kscl = const.tile([P, D], U8, name="kscl", align_bytes=64)
 
         def kgroup():
-            nc.vector.tensor_copy(out=kgrp[:].rearrange("p (c i) t -> p c t i", i=4),
-                                  in_=kraw[:].rearrange("p t (c i) -> p c t i", i=4))
+            nc.scalar.copy(out=kgrp[:].rearrange("p (c i) t -> p c t i", i=4),
+                           in_=kraw[:].rearrange("p t (c i) -> p c t i", i=4))
 
         def kquant():
             nc.vector.quantize_mx(
@@ -280,7 +281,6 @@ def tile_crosschannelinterp_t_kernel(tc, x, kernel, out):
         def live(q):
             return 0 <= q < NPAIR
 
-        LATE = NPAIR - 3
 
         intensity(0)
         for level in range(5):
@@ -360,11 +360,11 @@ def tile_crosschannelinterp_t_kernel(tc, x, kernel, out):
                 mult(s, 1)
             smooth(s - 1, 0)
             smooth(s - 1, 1)
-            if s - 1 >= SPLIT:
+            if s - 1 in SPLIT:
                 store(s - 1, 0, 2, 0, 2 * D)
             if 0 <= s - 2 < LATE:
                 ytrans(nc.gpsimd, s - 2, 0, 2, 0, GY)
-                store(s - 2, 0, 2, 2 * D if s - 2 >= SPLIT else 0, 3 * D)
+                store(s - 2, 0, 2, 2 * D if s - 2 in SPLIT else 0, 3 * D)
             if len(slots) > 2:
                 tree(*slots.pop(0))
             if live(s):
@@ -375,7 +375,7 @@ def tile_crosschannelinterp_t_kernel(tc, x, kernel, out):
                 tree(*slots[0])
             if s - 1 >= LATE:
                 ytrans(nc.vector, s - 1, 0, 2, 0, D)
-                store(s - 1, 0, 2, 2 * D, 3 * D)
+                store(s - 1, 0, 2, 0, 3 * D)
             else:
                 ytrans(nc.vector, s - 1, 0, 2, GY, D)
             if len(slots) > 1:

@@ -24,7 +24,6 @@ FLOPS = 2 * NB * T * D * D
 
 
 LATE = NPAIR - 3
-SPLIT = range(NPAIR // 2, LATE)
 GY = 256
 
 
@@ -274,9 +273,9 @@ def tile_crosschannelinterp_t_kernel(tc, x, kernel, out):
             eng.tensor_tensor(out=ob[:, a0:a1, 2 * D + c0:2 * D + c1], in0=ob_in[b][:, j0 + a0:j0 + a1, c0:c1],
                               in1=ob[:, a0:a1, c0:c1], op=ALU.subtract)
 
-        def store(q, a0, a1, c0, c1):
+        def store(q):
             b, j0 = q // 4, 2 * (q % 4)
-            nc.sync.dma_start(out=ov[b][:, j0 + a0:j0 + a1, c0:c1], in_=ob_t[q][:, a0:a1, c0:c1])
+            nc.sync.dma_start(out=ov[b][:, j0:j0 + 2, :], in_=ob_t[q][:])
 
         def live(q):
             return 0 <= q < NPAIR
@@ -360,11 +359,9 @@ def tile_crosschannelinterp_t_kernel(tc, x, kernel, out):
                 mult(s, 1)
             smooth(s - 1, 0)
             smooth(s - 1, 1)
-            if s - 1 in SPLIT:
-                store(s - 1, 0, 2, 0, 2 * D)
             if 0 <= s - 2 < LATE:
                 ytrans(nc.gpsimd, s - 2, 0, 2, 0, GY)
-                store(s - 2, 0, 2, 2 * D if s - 2 in SPLIT else 0, 3 * D)
+                store(s - 2)
             if len(slots) > 2:
                 tree(*slots.pop(0))
             if live(s):
@@ -375,7 +372,7 @@ def tile_crosschannelinterp_t_kernel(tc, x, kernel, out):
                 tree(*slots[0])
             if s - 1 >= LATE:
                 ytrans(nc.vector, s - 1, 0, 2, 0, D)
-                store(s - 1, 0, 2, 0, 3 * D)
+                store(s - 1)
             else:
                 ytrans(nc.vector, s - 1, 0, 2, GY, D)
             if len(slots) > 1:

from contextlib import ExitStack

import concourse.mybir as mybir
from concourse.masks import make_identity

FP8X4 = mybir.dt.float8_e4m3fn_x4
BF16 = mybir.dt.bfloat16
F32 = mybir.dt.float32
U32 = mybir.dt.uint32
U8 = mybir.dt.uint8
ALU = mybir.AluOpType
ACT = mybir.ActivationFunctionType
AX = mybir.AxisListType

NB, T, D = 4, 1024, 512
P = 128
J = T // P
KT = D // P
NPAIR = NB * J // 2
NQUAD = NB * J // 4
ONES_N = 32

FLOPS = 2 * NB * T * D * D


LATE = NPAIR - 3
GY = 256


def tile_crosschannelinterp_t_kernel(tc, x, kernel, out):
    nc = tc.nc
    with ExitStack() as ctx:
        const = ctx.enter_context(tc.tile_pool(name="const", bufs=1))
        xpool = ctx.enter_context(tc.tile_pool(name="xpool", bufs=1))
        opool = ctx.enter_context(tc.tile_pool(name="opool", bufs=6))
        epool = ctx.enter_context(tc.tile_pool(name="epool", bufs=3))
        work = ctx.enter_context(tc.tile_pool(name="work", bufs=2))
        stat = ctx.enter_context(tc.tile_pool(name="stat", bufs=4))
        ps_mean = ctx.enter_context(tc.psum_pool(name="ps_mean", bufs=1))
        ps_yt = ctx.enter_context(tc.psum_pool(name="ps_yt", bufs=2))
        ps_sm = ctx.enter_context(tc.psum_pool(name="ps_sm", bufs=3))
        ps_p = ctx.enter_context(tc.psum_pool(name="ps_p", bufs=2))
        ctx.enter_context(tc.manual_schedule())

        xv = [x[b].rearrange("(p j) c -> p j c", j=J) for b in range(NB)]
        ov = [out[b].rearrange("(p j) c -> p j c", j=J) for b in range(NB)]

        kraw = const.tile([P, KT, D], BF16, name="kraw")
        first = [xpool.tile([P, J, D], BF16, name="first%d" % i) for i in range(3)]
        xb = [None] + [xpool.tile([P, J, 3 * D], BF16, name="x%d" % b) for b in range(1, NB)]

        def block(b, i):
            return first[i][:] if b == 0 else xb[b][:, :, i * D:(i + 1) * D]

        yb = [block(b, 0) for b in range(NB)]
        wb = [block(b, 1) for b in range(NB)]
        ob_in = [block(b, 2) for b in range(NB)]

        def load_first(i, j0, j1):
            nc.sync.dma_start(out=first[i][:, j0:j1, :], in_=xv[0][:, j0:j1, i * D:(i + 1) * D])

        def load(b, j0, j1):
            nc.sync.dma_start(out=xb[b][:, j0:j1, :], in_=xv[b][:, j0:j1, :])

        load_first(1, 0, 2)
        load_first(0, 0, 4)
        load_first(0, 4, 8)
        load_first(1, 2, 4)
        load_first(1, 4, 8)
        nc.sync.dma_start(out=kraw[:], in_=kernel.rearrange("(p t) n -> p t n", t=KT))
        load(1, 0, 4)
        load_first(2, 0, 4)
        load(1, 4, 8)
        load_first(2, 4, 8)
        for b in range(2, NB):
            load(b, 0, 8)

        ident_f = const.tile([P, P], F32, name="ident_f")
        make_identity(nc, ident_f[:])
        ones = const.tile([P, ONES_N], BF16, name="ones")
        nc.vector.memset(ones[:], 1.0 / T)

        kgrp = const.tile([P, D, KT], BF16, name="kgrp", align_bytes=64)
        kcodes = const.tile([P, D], U32, name="kcodes", align_bytes=64)
        kscl = const.tile([P, D], U8, name="kscl", align_bytes=64)

        def kgroup():
            nc.scalar.copy(out=kgrp[:].rearrange("p (c i) t -> p c t i", i=4),
                           in_=kraw[:].rearrange("p t (c i) -> p c t i", i=4))

        def kquant():
            nc.vector.quantize_mx(
                out=kcodes[:].bitcast(FP8X4),
                scales=kscl[:],
                in_=kgrp[:].rearrange("p n t -> p (n t)"),
            )

        msum_t = {}
        negmean = {}
        mbc_t = {}
        negmean_sb = {}
        tree_t = {}
        negmax = {}
        yt_t = {}
        dt_t = {}
        e_t = {}
        ssum_t = {}
        rs_t = {}
        sm_t = {}
        grp_t = {}
        cod_t = {}
        ob_t = {}
        pp_t = {}

        def mean_mm(b, half):
            if half == 0:
                msum_t[b] = ps_mean.tile([P, 2, KT, ONES_N], F32, name="msum", tag="mean")
            for t in range(KT):
                for j in range(4 * half, 4 * half + 4):
                    nc.tensor.matmul(
                        out=msum_t[b][:, half, t, :],
                        lhsT=yb[b][:, j, t:D:KT],
                        rhs=ones[:],
                        start=(j == 4 * half),
                        stop=(j == 4 * half + 3),
                    )

        def neg_mean(b):
            nm = stat.tile([P, KT], F32, name="negmean")
            nc.vector.tensor_reduce(out=nm[:], in_=msum_t[b][:, :, :, 0].rearrange("p h t -> p t h"),
                                    axis=AX.X, op=ALU.add, negate=True)
            negmean[b] = nm

        def mean_tr(b):
            mbc = ps_mean.tile([P, KT, P], F32, name="mbc", tag="mean")
            for t in range(KT):
                nc.tensor.transpose(mbc[:, t, :], negmean[b][:, t:t + 1].to_broadcast([P, P]), ident_f[:])
            mbc_t[b] = mbc

        def mean_copy(b):
            msb = work.tile([P, D], F32, name="msb")
            nc.scalar.copy(out=msb[:].rearrange("p (c i t) -> p c t i", i=4, t=KT), in_=mbc_t[b][:].rearrange("p t (c i) -> p c t i", i=4))
            negmean_sb[b] = msb

        def ytr(h, u):
            b, j0 = h // 2, 4 * (h % 2)
            yt = ps_yt.tile([P, 4 * P], F32, name="yt")
            for a4 in range(4):
                words = yb[b][:, j0 + a4, 0:D].bitcast(F32)
                nc.tensor.transpose(yt[:, a4 * P:(a4 + 1) * P], words[:, u:D // 2:2], ident_f[:])
            yt_t[(h, u)] = yt

        def centre(h, t, on_vector=False):
            b = h // 2
            if t == 0:
                dt_t[h] = work.tile([P, KT, 4 * P], F32, name="dT")
            src = yt_t[(h, t // 2)][:].bitcast(BF16).rearrange("p (r e) -> p e r", e=2)[:, t % 2, :]
            if on_vector:
                nc.vector.tensor_scalar(out=dt_t[h][:, t, :], in0=src,
                                        scalar1=negmean[b][:, t:t + 1], scalar2=None, op0=ALU.add)
            else:
                nc.scalar.activation(out=dt_t[h][:, t, :], in_=src, func=ACT.Identity,
                                     bias=negmean[b][:, t:t + 1], scale=1.0)

        def centre_two(h, u):
            for t in (2 * u, 2 * u + 1):
                centre(h, t)

        def tree(h, level, half=None):
            b, j0, n = h // 2, 4 * (h % 2), 4
            if half is not None:
                j0, n = j0 + 2 * half, 2
            if level == 0:
                t1 = work.tile([P, 4, 256], BF16, name="t1")
                nc.vector.tensor_tensor(out=t1[:, 0:n, :], in0=wb[b][:, j0:j0 + n, 0:256],
                                        in1=wb[b][:, j0:j0 + n, 256:D], op=ALU.max)
                tree_t[h] = t1
            elif level < 4:
                w = 256 >> level
                src = tree_t[h]
                dst = work.tile([P, 4, w], BF16, name="t%d" % (level + 1))
                nc.vector.tensor_tensor(out=dst[:, 0:n, :], in0=src[:, 0:n, 0:w], in1=src[:, 0:n, w:2 * w],
                                        op=ALU.max)
                tree_t[h] = dst
            else:
                nm = stat.tile([P, 4], F32, name="nm")
                nc.vector.tensor_reduce(out=nm[:, 0:n], in_=tree_t[h][:, 0:n, :], axis=AX.X, op=ALU.max, negate=True)
                for i in range(n // 2):
                    negmax[4 * b + j0 // 2 + i] = nm[:, 2 * i:2 * i + 2]

        def expo(q):
            b, j0 = q // 4, 2 * (q % 4)
            e_t[q] = epool.tile([P, 2, D], F32, name="e")
            ssum_t[q] = stat.tile([P, 2], F32, name="ssum")
            for a in range(2):
                nc.scalar.activation(
                    out=e_t[q][:, a, :].rearrange("p (t c i) -> p c t i", t=KT, i=4),
                    in_=wb[b][:, j0 + a, :].rearrange("p (c i t) -> p c t i", i=4, t=KT),
                    func=ACT.Exp,
                    bias=negmax[q][:, a:a + 1], scale=1.0, accum_out=ssum_t[q][:, a:a + 1],
                )

        def recip(q):
            rs = stat.tile([P, 2], F32, name="rs")
            nc.vector.reciprocal(out=rs[:], in_=ssum_t[q][:])
            rs_t[q] = rs

        def norm(q, a):
            if q < 2 or (a == 1 and q % 2 == 1):
                nc.vector.tensor_scalar(out=e_t[q][:, a, :], in0=e_t[q][:, a, :], scalar1=rs_t[q][:, a:a + 1],
                                        scalar2=None, op0=ALU.mult)
            elif a == 0:
                nc.gpsimd.tensor_scalar(out=e_t[q][:, a, :], in0=e_t[q][:, a, :], scalar1=rs_t[q][:, a:a + 1],
                                        scalar2=0.0, op0=ALU.mult, op1=ALU.add)
            else:
                nc.scalar.activation(out=e_t[q][:, a, :], in_=e_t[q][:, a, :], func=ACT.Copy,
                                     scale=rs_t[q][:, a:a + 1])

        def smtr(q, a):
            sm = ps_sm.tile([P, KT, P], F32, name="sm")
            for t in range(KT):
                nc.tensor.transpose(sm[:, t, :], e_t[q][:, a, t * P:(t + 1) * P], ident_f[:])
            sm_t[(q, a)] = sm

        def mult(q, a):
            h = q // 2
            if a == 0:
                grp_t[q] = work.tile([P, 2, P, KT], BF16, name="grp", align_bytes=64)
            c0 = (2 * (q % 2) + a) * P
            nc.vector.tensor_tensor(
                out=grp_t[q][:, a, :, :].rearrange("p (c i) t -> p c t i", i=4),
                in0=dt_t[h][:, :, c0:c0 + P].rearrange("p t (c i) -> p c t i", i=4),
                in1=sm_t[(q, a)][:].rearrange("p t (c i) -> p c t i", i=4),
                op=ALU.mult,
            )

        def quant(q):
            codes = work.tile([P, 2 * P], U32, name="codes", align_bytes=64)
            scl = work.tile([P, 2 * P], U8, name="scl", align_bytes=64)
            nc.vector.quantize_mx(
                out=codes[:].bitcast(FP8X4), scales=scl[:],
                in_=grp_t[q][:].rearrange("p a r t -> p (a r t)"),
            )
            cod_t[q] = (codes, scl)

        def mxmm(q):
            codes, scl = cod_t[q]
            for a in range(2):
                pp = ps_p.tile([P, D], F32, name="pp")
                nc.tensor.matmul_mx(
                    out=pp[:],
                    lhsT=codes[:, a * P:(a + 1) * P].bitcast(FP8X4),
                    lhsT_scale=scl[:, a * P:(a + 1) * P],
                    rhs=kcodes[:].bitcast(FP8X4),
                    rhs_scale=kscl[:],
                    start=True, stop=True,
                )
                pp_t[(q, a)] = pp

        def intensity(q):
            b, j0 = q // 4, 2 * (q % 4)
            ob = opool.tile([P, 2, 3 * D], F32, name="ob")
            nc.scalar.activation(out=ob[:, :, D:2 * D], in_=wb[b][:, j0:j0 + 2, :], func=ACT.Exp)
            ob_t[q] = ob

        def smooth(q, a):
            nc.vector.tensor_tensor(out=ob_t[q][:, a, 0:D], in0=pp_t[(q, a)][:], in1=negmean_sb[q // 4][:],
                                    op=ALU.subtract)

        def ytrans(eng, q, a0, a1, c0, c1):
            b, j0 = q // 4, 2 * (q % 4)
            ob = ob_t[q]
            eng.tensor_tensor(out=ob[:, a0:a1, 2 * D + c0:2 * D + c1], in0=ob_in[b][:, j0 + a0:j0 + a1, c0:c1],
                              in1=ob[:, a0:a1, c0:c1], op=ALU.subtract)

        def store(q):
            b, j0 = q // 4, 2 * (q % 4)
            nc.sync.dma_start(out=ov[b][:, j0:j0 + 2, :], in_=ob_t[q][:])

        def live(q):
            return 0 <= q < NPAIR


        intensity(0)
        for level in range(5):
            tree(0, level, 0)
        expo(0)
        mean_mm(0, 0)
        mean_mm(0, 1)
        ytr(0, 0)
        ytr(0, 1)
        tree(0, 0, 1)
        neg_mean(0)
        tree(0, 1, 1)
        recip(0)
        norm(0, 0)
        norm(0, 1)
        for level in range(2, 5):
            tree(0, level, 1)
        centre_two(0, 0)
        centre(0, 2)
        centre(0, 3, on_vector=True)
        smtr(0, 0)
        smtr(0, 1)
        expo(1)
        ytr(1, 0)
        mean_tr(0)
        mean_copy(0)

        mult(0, 0)
        mult(0, 1)
        centre_two(1, 0)
        recip(1)
        norm(1, 0)
        tree(1, 0)
        norm(1, 1)
        smtr(1, 0)
        tree(1, 1)
        quant(0)
        tree(1, 2)
        tree(2, 0)
        tree(1, 3)
        tree(2, 1)
        tree(1, 4)
        kgroup()
        kquant()
        expo(2)
        ytr(1, 1)
        mean_mm(1, 0)
        smtr(1, 1)
        mxmm(0)

        for s in range(1, NPAIR + 1):
            slots = []
            if s % 2 == 0 and (s + 4) // 2 < NQUAD:
                slots = [((s + 4) // 2, 0), ((s + 4) // 2, 1)]
            if s % 2 == 1 and (s + 3) // 2 < NQUAD:
                slots = [((s + 3) // 2, 2), ((s + 3) // 2, 3), ((s + 3) // 2, 4)]
            bn = (s + 2) // 4
            new_mean = s % 4 == 2 and bn < NB

            if live(s + 1):
                recip(s + 1)
                norm(s + 1, 0)
            if new_mean:
                neg_mean(bn)
            if s % 4 == 3 and (s + 1) // 4 < NB:
                mean_copy((s + 1) // 4)
            if live(s + 2):
                expo(s + 2)
            if s % 2 == 1 and live(s + 1):
                norm(s + 1, 1)
            if s % 2 == 0 and (s + 2) // 2 < NQUAD:
                centre_two((s + 2) // 2, 0)
            if s % 2 == 1 and (s + 1) // 2 < NQUAD:
                centre_two((s + 1) // 2, 1)
            if live(s):
                mult(s, 0)
                mult(s, 1)
            smooth(s - 1, 0)
            smooth(s - 1, 1)
            if 0 <= s - 2 < LATE:
                ytrans(nc.gpsimd, s - 2, 0, 2, 0, GY)
                store(s - 2)
            if len(slots) > 2:
                tree(*slots.pop(0))
            if live(s):
                quant(s)
            if s % 2 == 0 and s < NPAIR - 1:
                norm(s + 1, 1)
            if len(slots) > 0:
                tree(*slots[0])
            if s - 1 >= LATE:
                ytrans(nc.vector, s - 1, 0, 2, 0, D)
                store(s - 1)
            else:
                ytrans(nc.vector, s - 1, 0, 2, GY, D)
            if len(slots) > 1:
                tree(*slots[1])
            if s < NPAIR - 2:
                intensity(s)
            elif s == NPAIR - 2:
                intensity(s)
                intensity(s + 1)
            if s % 2 == 1 and 2 <= (s + 3) // 2 < NQUAD:
                ytr((s + 3) // 2, 0)
            if s % 2 == 0 and (s + 2) // 2 < NQUAD:
                ytr((s + 2) // 2, 1)
            if live(s + 1):
                smtr(s + 1, 0)
            if s % 4 == 0 and (s + 4) // 4 < NB:
                mean_mm((s + 4) // 4, 0)
            if s % 4 == 1 and (s + 3) // 4 < NB:
                mean_mm((s + 3) // 4, 1)
            if new_mean:
                mean_tr(bn)
            if live(s + 1):
                smtr(s + 1, 1)
            if live(s):
                mxmm(s)
